import numpy as np
import ml_dtypes

BF16 = ml_dtypes.bfloat16


def bf(x):
    return np.asarray(x, np.float32).astype(BF16)


def f32(x):
    return np.asarray(x, np.float32)


def f64(x):
    return np.asarray(x).astype(np.float64)


def striped(idx):
    return np.tile(idx.reshape(-1, 16).T, (8, 1))


C, S, N, H, DH = 512, 2048, 1024, 4, 128
EPS = 1e-5


def setup_inputs():
    return {
        "emb": f32(0.1 * np.random.standard_normal((C, S))),
        "pos": f32(np.random.standard_normal((C, N))),
        "ln_w": f32(1.0 + 0.1 * np.random.standard_normal((C, 1))),
        "ln_b": f32(0.1 * np.random.standard_normal((C, 1))),
        "wq": bf(1.5 * np.random.standard_normal((C, C)) / np.sqrt(C)),
        "bq": f32(0.3 * np.random.standard_normal((C, 1))),
        "wk": bf(1.5 * np.random.standard_normal((C, C)) / np.sqrt(C)),
        "wv": bf(np.random.standard_normal((C, C)) / np.sqrt(C)),
        "bv": f32(0.2 * np.random.standard_normal((C, 1))),
        "wo": bf(2.0 * np.random.standard_normal((C, C)) / np.sqrt(C)),
        "bo": f32(0.2 * np.random.standard_normal((C, 1))),
        "offs": striped(np.random.permutation(np.tile(np.arange(S), 2))[:N]),
    }


def reference(emb, pos, ln_w, ln_b, wq, bq, wk, wv, bv, wo, bo, offs):
    idx = offs[:16].T.reshape(-1)
    x0 = (np.sqrt(C) * f64(emb))[:, idx] + f64(pos)
    mu = x0.mean(axis=0, keepdims=True)
    var = ((x0 - mu) ** 2).mean(axis=0, keepdims=True)
    h = f64(ln_w) * (x0 - mu) / np.sqrt(var + EPS) + f64(ln_b)
    q = (f64(wq).T @ h + f64(bq)).reshape(H, DH, N)
    k = (f64(wk).T @ h).reshape(H, DH, N)
    v = (f64(wv).T @ h + f64(bv)).reshape(H, DH, N)
    sc = (q.transpose(0, 2, 1) @ k) / np.sqrt(DH)
    e = np.exp(sc)
    a = e / e.sum(axis=2, keepdims=True)
    o = (v @ a.transpose(0, 2, 1)).reshape(C, N)
    return x0 + f64(wo).T @ o + f64(bo)

@@ -1,0 +1,228 @@
+import math
+
+import concourse.mybir as mybir
+from concourse.masks import make_identity
+
+F32 = mybir.dt.float32
+BF16 = mybir.dt.bfloat16
+U16 = mybir.dt.uint16
+ALU = mybir.AluOpType
+ACT = mybir.ActivationFunctionType
+
+P = 128
+C, S, N, H, DH = 512, 2048, 1024, 4, 128
+EPS = 1e-5
+CB = C // P
+HALF = 512
+NH = N // HALF
+TB = N // P
+QB = HALF // P
+FLOPS = 2 * (4 * C * C * N + 2 * H * N * N * DH)
+
+
+def tile_transformerencoder_b_kernel(
+    tc, emb, pos, ln_w, ln_b, wq, bq, wk, wv, bv, wo, bo, offs, out
+):
+    nc = tc.nc
+    with (
+        tc.tile_pool(name="lists", bufs=1) as lists,
+        tc.tile_pool(name="held", bufs=1) as held,
+        tc.tile_pool(name="work", bufs=3) as work,
+        tc.tile_pool(name="probs", bufs=2) as probs,
+        tc.psum_pool(name="acc", bufs=2) as acc,
+        tc.psum_pool(name="score", bufs=3) as score,
+        tc.psum_pool(name="ctx", bufs=2) as ctx,
+        tc.psum_pool(name="flip", bufs=1) as flip,
+    ):
+        offsets = lists.tile([P, N // 16], U16, name="offsets")
+        nc.sync.dma_start(offsets[:], offs)
+
+        table = [held.tile([P, S], F32, name=f"table{b}") for b in range(CB)]
+        pos_sb = [held.tile([P, N], F32, name=f"pos{b}") for b in range(CB)]
+        for b in range(CB):
+            nc.sync.dma_start(pos_sb[b][:], pos[b * P : (b + 1) * P, :])
+            nc.sync.dma_start(table[b][:], emb[b * P : (b + 1) * P, :])
+
+        per_channel = {}
+        with nc.allow_non_contiguous_dma(reason="512 floats, one to a partition"):
+            for name, vec in (("ln_w", ln_w), ("ln_b", ln_b), ("bq", bq), ("bo", bo)):
+                per_channel[name] = held.tile([P, CB], F32, name=name)
+                nc.sync.dma_start(
+                    per_channel[name][:], vec.rearrange("(b p) o -> p (b o)", p=P)
+                )
+        bv_row = held.tile([P, C], F32, name="bv_row")
+        nc.sync.dma_start(bv_row[:], bv.rearrange("c o -> (c o)").partition_broadcast(P))
+
+        weights = {}
+        for name, w in (("q", wq), ("k", wk), ("v", wv), ("o", wo)):
+            weights[name] = held.tile([P, CB, C], BF16, name=f"w{name}")
+            nc.sync.dma_start(weights[name][:], w.rearrange("(b p) m -> p b m", p=P))
+
+        mean_w = held.tile([P, P], F32, name="mean_w")
+        nc.vector.memset(mean_w[:], 1.0 / C)
+        eps = held.tile([P, 1], F32, name="eps")
+        nc.vector.memset(eps[:], EPS)
+        ident = held.tile([P, P], BF16, name="ident")
+        make_identity(nc, ident[:])
+        v_aug = [held.tile([P, H, DH + 1], BF16, name=f"v_aug{i}") for i in range(TB)]
+        for i in range(TB):
+            nc.gpsimd.memset(v_aug[i][:], 1.0)
+
+        x0 = [held.tile([P, N], F32, name=f"x0_{b}") for b in range(CB)]
+        mu_ps = [acc.tile([P, HALF], F32, name=f"mu_ps{s}", tag="acc") for s in range(NH)]
+        for b in range(CB):
+            nc.scalar.mul(table[b][:], table[b][:], math.sqrt(C))
+            for s in range(NH):
+                cols = slice(s * HALF, (s + 1) * HALF)
+                piece = offsets[:, s * HALF // 16 : (s + 1) * HALF // 16]
+                nc.vector.tensor_tensor(
+                    x0[b][:, cols], table[b][:].indirect(piece), pos_sb[b][:, cols], ALU.add
+                )
+                nc.tensor.matmul(
+                    mu_ps[s][:], mean_w[:], x0[b][:, cols], start=(b == 0), stop=(b == CB - 1)
+                )
+
+        xc = [held.tile([P, N], F32, name=f"xc{b}") for b in range(CB)]
+        rstd = held.tile([P, N], F32, name="rstd")
+        h = [held.tile([P, N], BF16, name=f"h{b}") for b in range(CB)]
+        for s in range(NH):
+            cols = slice(s * HALF, (s + 1) * HALF)
+            var_ps = score.tile([P, HALF], F32, name="var_ps", tag="score")
+            for b in range(CB):
+                nc.vector.tensor_tensor(xc[b][:, cols], x0[b][:, cols], mu_ps[s][:], ALU.subtract)
+                sq = work.tile([P, HALF], F32, name="sq")
+                nc.scalar.activation(sq[:], xc[b][:, cols], ACT.Square)
+                nc.tensor.matmul(var_ps[:], mean_w[:], sq[:], start=(b == 0), stop=(b == CB - 1))
+            nc.scalar.activation(rstd[:, cols], var_ps[:], ACT.Abs_reciprocal_sqrt, bias=eps[:])
+        for s in range(NH):
+            cols = slice(s * HALF, (s + 1) * HALF)
+            for b in range(CB):
+                xn = work.tile([P, HALF], F32, name="xn")
+                nc.vector.tensor_tensor(xn[:], xc[b][:, cols], rstd[:, cols], ALU.mult)
+                nc.scalar.activation(
+                    h[b][:, cols],
+                    xn[:],
+                    ACT.Identity,
+                    bias=per_channel["ln_b"][:, b : b + 1],
+                    scale=per_channel["ln_w"][:, b : b + 1],
+                )
+
+        q = [held.tile([P, N], BF16, name=f"q{t}") for t in range(H)]
+        k = [held.tile([P, N], BF16, name=f"k{t}") for t in range(H)]
+        o = [held.tile([P, N], BF16, name=f"o{t}") for t in range(H)]
+
+        def project(w, t, s):
+            ps = acc.tile([P, HALF], F32, name="proj_ps", tag="acc")
+            for b in range(CB):
+                nc.tensor.matmul(
+                    ps[:],
+                    w[:, b, t * DH : (t + 1) * DH],
+                    h[b][:, s * HALF : (s + 1) * HALF],
+                    start=(b == 0),
+                    stop=(b == CB - 1),
+                )
+            return ps
+
+        def project_q(t, s):
+            ps = project(weights["q"], t, s)
+            nc.vector.tensor_scalar_add(
+                q[t][:, s * HALF : (s + 1) * HALF], ps[:], per_channel["bq"][:, t : t + 1]
+            )
+
+        def project_k(t, s):
+            ps = project(weights["k"], t, s)
+            nc.scalar.copy(k[t][:, s * HALF : (s + 1) * HALF], ps[:])
+
+        def project_v(i):
+            ps = acc.tile([P, C], F32, name="v_ps", tag="acc")
+            for b in range(CB):
+                nc.tensor.matmul(
+                    ps[:],
+                    h[b][:, i * P : (i + 1) * P],
+                    weights["v"][:, b, :],
+                    start=(b == 0),
+                    stop=(b == CB - 1),
+                )
+            nc.vector.tensor_tensor(
+                v_aug[i][:, :, 0:DH],
+                ps[:].rearrange("p (t d) -> p t d", t=H),
+                bv_row[:].rearrange("p (t d) -> p t d", t=H),
+                ALU.add,
+            )
+
+        def exp_scores(t, s, i, e):
+            ps = score.tile([P, HALF], F32, name="sc_ps", tag="score")
+            nc.tensor.matmul(
+                ps[:],
+                k[t][:, i * P : (i + 1) * P],
+                q[t][:, s * HALF : (s + 1) * HALF],
+                start=True,
+                stop=True,
+            )
+            nc.scalar.activation(e[:, i, :], ps[:], ACT.Exp, scale=1.0 / math.sqrt(DH))
+
+        def attend(t, j, e):
+            ps = ctx.tile([P, DH + 1], F32, name="ctx_ps", tag="ctx")
+            for i in range(TB):
+                nc.tensor.matmul(
+                    ps[:],
+                    e[:, i, j * P : (j + 1) * P],
+                    v_aug[i][:, t, :],
+                    start=(i == 0),
+                    stop=(i == TB - 1),
+                )
+            rsum = work.tile([P, 1], F32, name="rsum")
+            nc.vector.reciprocal(rsum[:], ps[:, DH : DH + 1])
+            o_tok = work.tile([P, DH], BF16, name="o_tok")
+            nc.vector.tensor_scalar_mul(o_tok[:], ps[:, 0:DH], rsum[:])
+            return o_tok
+
+        def project_out(m, s):
+            cols = slice(s * HALF, (s + 1) * HALF)
+            ps = acc.tile([P, HALF], F32, name="y_ps", tag="acc")
+            for t in range(H):
+                nc.tensor.matmul(
+                    ps[:],
+                    weights["o"][:, t, m * P : (m + 1) * P],
+                    o[t][:, cols],
+                    start=(t == 0),
+                    stop=(t == H - 1),
+                )
+            y = work.tile([P, HALF], F32, name="y")
+            nc.vector.scalar_tensor_tensor(
+                y[:], ps[:], per_channel["bo"][:, m : m + 1], x0[m][:, cols], ALU.add, ALU.add
+            )
+            nc.sync.dma_start(out[m * P : (m + 1) * P, cols], y[:])
+
+        groups = [(t, s) for s in range(NH) for t in range(H)]
+        e_now = None
+        for g in range(-1, len(groups)):
+            e_next = None
+            if g + 1 < len(groups):
+                t_next, s_next = groups[g + 1]
+                project_q(t_next, s_next)
+                if s_next == 0:
+                    for s in range(NH):
+                        project_k(t_next, s)
+                e_next = probs.tile([P, TB, HALF], BF16, name="e")
+            if g >= H:
+                project_out(g - H, 0)
+            if g >= 0:
+                flip_ps = flip.tile([P, HALF], BF16, name="flip_ps", tag="flip")
+            for j in range(QB):
+                if g < 0:
+                    project_v(2 * j)
+                    project_v(2 * j + 1)
+                else:
+                    o_tok = attend(groups[g][0], j, e_now)
+                if e_next is not None:
+                    exp_scores(t_next, s_next, 2 * j, e_next)
+                    exp_scores(t_next, s_next, 2 * j + 1, e_next)
+                if g >= 0:
+                    nc.tensor.transpose(flip_ps[:, j * P : (j + 1) * P], o_tok[:], ident[:])
+            if g >= 0:
+                t, s = groups[g]
+                nc.vector.tensor_copy(o[t][:, s * HALF : (s + 1) * HALF], flip_ps[:])
+            e_now = e_next
+        for m in range(CB):
+            project_out(m, 1)

@@ -40,8 +40,8 @@ def tile_transformerencoder_b_kernel(
         table = [held.tile([P, S], F32, name=f"table{b}") for b in range(CB)]
         pos_sb = [held.tile([P, N], F32, name=f"pos{b}") for b in range(CB)]
         for b in range(CB):
-            nc.sync.dma_start(pos_sb[b][:], pos[b * P : (b + 1) * P, :])
             nc.sync.dma_start(table[b][:], emb[b * P : (b + 1) * P, :])
+            nc.sync.dma_start(pos_sb[b][:], pos[b * P : (b + 1) * P, :])
 
         per_channel = {}
         with nc.allow_non_contiguous_dma(reason="512 floats, one to a partition"):
@@ -71,7 +71,8 @@ def tile_transformerencoder_b_kernel(
         x0 = [held.tile([P, N], F32, name=f"x0_{b}") for b in range(CB)]
         mu_ps = [acc.tile([P, HALF], F32, name=f"mu_ps{s}", tag="acc") for s in range(NH)]
         for b in range(CB):
-            nc.scalar.mul(table[b][:], table[b][:], math.sqrt(C))
+            nc.scalar.mul(table[b][:, 0 : S // 2], table[b][:, 0 : S // 2], math.sqrt(C))
+            nc.vector.tensor_scalar_mul(table[b][:, S // 2 : S], table[b][:, S // 2 : S], math.sqrt(C))
             for s in range(NH):
                 cols = slice(s * HALF, (s + 1) * HALF)
                 piece = offsets[:, s * HALF // 16 : (s + 1) * HALF // 16]
@@ -85,17 +86,17 @@ def tile_transformerencoder_b_kernel(
         xc = [held.tile([P, N], F32, name=f"xc{b}") for b in range(CB)]
         rstd = held.tile([P, N], F32, name="rstd")
         h = [held.tile([P, N], BF16, name=f"h{b}") for b in range(CB)]
+        var_ps = [score.tile([P, HALF], F32, name=f"var_ps{s}", tag="score") for s in range(NH)]
         for s in range(NH):
             cols = slice(s * HALF, (s + 1) * HALF)
-            var_ps = score.tile([P, HALF], F32, name="var_ps", tag="score")
             for b in range(CB):
                 nc.vector.tensor_tensor(xc[b][:, cols], x0[b][:, cols], mu_ps[s][:], ALU.subtract)
                 sq = work.tile([P, HALF], F32, name="sq")
                 nc.scalar.activation(sq[:], xc[b][:, cols], ACT.Square)
-                nc.tensor.matmul(var_ps[:], mean_w[:], sq[:], start=(b == 0), stop=(b == CB - 1))
-            nc.scalar.activation(rstd[:, cols], var_ps[:], ACT.Abs_reciprocal_sqrt, bias=eps[:])
+                nc.tensor.matmul(var_ps[s][:], mean_w[:], sq[:], start=(b == 0), stop=(b == CB - 1))
         for s in range(NH):
             cols = slice(s * HALF, (s + 1) * HALF)
+            nc.scalar.activation(rstd[:, cols], var_ps[s][:], ACT.Abs_reciprocal_sqrt, bias=eps[:])
             for b in range(CB):
                 xn = work.tile([P, HALF], F32, name="xn")
                 nc.vector.tensor_tensor(xn[:], xc[b][:, cols], rstd[:, cols], ALU.mult)
@@ -194,8 +195,14 @@ def tile_transformerencoder_b_kernel(
             )
             nc.sync.dma_start(out[m * P : (m + 1) * P, cols], y[:])
 
+        def flip_back(o_tok, t, s, j, flip_ps):
+            nc.tensor.transpose(flip_ps[:, j * P : (j + 1) * P], o_tok[:], ident[:])
+            if j == QB - 1:
+                nc.vector.tensor_copy(o[t][:, s * HALF : (s + 1) * HALF], flip_ps[:])
+
         groups = [(t, s) for s in range(NH) for t in range(H)]
         e_now = None
+        late = None
         for g in range(-1, len(groups)):
             e_next = None
             if g + 1 < len(groups):
@@ -205,10 +212,6 @@ def tile_transformerencoder_b_kernel(
                     for s in range(NH):
                         project_k(t_next, s)
                 e_next = probs.tile([P, TB, HALF], BF16, name="e")
-            if g >= H:
-                project_out(g - H, 0)
-            if g >= 0:
-                flip_ps = flip.tile([P, HALF], BF16, name="flip_ps", tag="flip")
             for j in range(QB):
                 if g < 0:
                     project_v(2 * j)
@@ -218,11 +221,15 @@ def tile_transformerencoder_b_kernel(
                 if e_next is not None:
                     exp_scores(t_next, s_next, 2 * j, e_next)
                     exp_scores(t_next, s_next, 2 * j + 1, e_next)
+                if late is not None:
+                    flip_back(*late)
                 if g >= 0:
-                    nc.tensor.transpose(flip_ps[:, j * P : (j + 1) * P], o_tok[:], ident[:])
-            if g >= 0:
-                t, s = groups[g]
-                nc.vector.tensor_copy(o[t][:, s * HALF : (s + 1) * HALF], flip_ps[:])
+                    if j == 0:
+                        flip_ps = flip.tile([P, HALF], BF16, name="flip_ps", tag="flip")
+                    late = (o_tok, groups[g][0], groups[g][1], j, flip_ps)
+            if g >= H:
+                project_out(g - H, 0)
             e_now = e_next
+        flip_back(*late)
         for m in range(CB):
             project_out(m, 1)

@@ -17,6 +17,7 @@ HALF = 512
 NH = N // HALF
 TB = N // P
 QB = HALF // P
+KEYS_A_STEP = TB // QB
 FLOPS = 2 * (4 * C * C * N + 2 * H * N * N * DH)
 
 
@@ -29,8 +30,7 @@ def tile_transformerencoder_b_kernel(
         tc.tile_pool(name="held", bufs=1) as held,
         tc.tile_pool(name="work", bufs=3) as work,
         tc.tile_pool(name="probs", bufs=2) as probs,
-        tc.psum_pool(name="acc", bufs=2) as acc,
-        tc.psum_pool(name="score", bufs=3) as score,
+        tc.psum_pool(name="banks", bufs=5) as banks,
         tc.psum_pool(name="ctx", bufs=2) as ctx,
         tc.psum_pool(name="flip", bufs=1) as flip,
     ):
@@ -69,7 +69,7 @@ def tile_transformerencoder_b_kernel(
             nc.gpsimd.memset(v_aug[i][:], 1.0)
 
         x0 = [held.tile([P, N], F32, name=f"x0_{b}") for b in range(CB)]
-        mu_ps = [acc.tile([P, HALF], F32, name=f"mu_ps{s}", tag="acc") for s in range(NH)]
+        mu_ps = [banks.tile([P, HALF], F32, name=f"mu_ps{s}", tag="bank") for s in range(NH)]
         for b in range(CB):
             nc.scalar.mul(table[b][:, 0 : S // 2], table[b][:, 0 : S // 2], math.sqrt(C))
             nc.vector.tensor_scalar_mul(table[b][:, S // 2 : S], table[b][:, S // 2 : S], math.sqrt(C))
@@ -86,7 +86,7 @@ def tile_transformerencoder_b_kernel(
         xc = [held.tile([P, N], F32, name=f"xc{b}") for b in range(CB)]
         rstd = held.tile([P, N], F32, name="rstd")
         h = [held.tile([P, N], BF16, name=f"h{b}") for b in range(CB)]
-        var_ps = [score.tile([P, HALF], F32, name=f"var_ps{s}", tag="score") for s in range(NH)]
+        var_ps = [banks.tile([P, HALF], F32, name=f"var_ps{s}", tag="bank") for s in range(NH)]
         for s in range(NH):
             cols = slice(s * HALF, (s + 1) * HALF)
             for b in range(CB):
@@ -113,7 +113,7 @@ def tile_transformerencoder_b_kernel(
         o = [held.tile([P, N], BF16, name=f"o{t}") for t in range(H)]
 
         def project(w, t, s):
-            ps = acc.tile([P, HALF], F32, name="proj_ps", tag="acc")
+            ps = banks.tile([P, HALF], F32, name="proj_ps", tag="bank")
             for b in range(CB):
                 nc.tensor.matmul(
                     ps[:],
@@ -124,18 +124,18 @@ def tile_transformerencoder_b_kernel(
                 )
             return ps
 
+        def project_k(t, s):
+            ps = project(weights["k"], t, s)
+            nc.vector.tensor_copy(k[t][:, s * HALF : (s + 1) * HALF], ps[:])
+
         def project_q(t, s):
             ps = project(weights["q"], t, s)
             nc.vector.tensor_scalar_add(
                 q[t][:, s * HALF : (s + 1) * HALF], ps[:], per_channel["bq"][:, t : t + 1]
             )
 
-        def project_k(t, s):
-            ps = project(weights["k"], t, s)
-            nc.scalar.copy(k[t][:, s * HALF : (s + 1) * HALF], ps[:])
-
         def project_v(i):
-            ps = acc.tile([P, C], F32, name="v_ps", tag="acc")
+            ps = banks.tile([P, C], F32, name="v_ps", tag="bank")
             for b in range(CB):
                 nc.tensor.matmul(
                     ps[:],
@@ -152,7 +152,7 @@ def tile_transformerencoder_b_kernel(
             )
 
         def exp_scores(t, s, i, e):
-            ps = score.tile([P, HALF], F32, name="sc_ps", tag="score")
+            ps = banks.tile([P, HALF], F32, name="sc_ps", tag="bank")
             nc.tensor.matmul(
                 ps[:],
                 k[t][:, i * P : (i + 1) * P],
@@ -178,9 +178,14 @@ def tile_transformerencoder_b_kernel(
             nc.vector.tensor_scalar_mul(o_tok[:], ps[:, 0:DH], rsum[:])
             return o_tok
 
+        def flip_back(o_tok, t, s, j, flip_ps):
+            nc.tensor.transpose(flip_ps[:, j * P : (j + 1) * P], o_tok[:], ident[:])
+            if j == QB - 1:
+                nc.vector.tensor_copy(o[t][:, s * HALF : (s + 1) * HALF], flip_ps[:])
+
         def project_out(m, s):
             cols = slice(s * HALF, (s + 1) * HALF)
-            ps = acc.tile([P, HALF], F32, name="y_ps", tag="acc")
+            ps = banks.tile([P, HALF], F32, name="y_ps", tag="bank")
             for t in range(H):
                 nc.tensor.matmul(
                     ps[:],
@@ -195,41 +200,48 @@ def tile_transformerencoder_b_kernel(
             )
             nc.sync.dma_start(out[m * P : (m + 1) * P, cols], y[:])
 
-        def flip_back(o_tok, t, s, j, flip_ps):
-            nc.tensor.transpose(flip_ps[:, j * P : (j + 1) * P], o_tok[:], ident[:])
-            if j == QB - 1:
-                nc.vector.tensor_copy(o[t][:, s * HALF : (s + 1) * HALF], flip_ps[:])
-
         groups = [(t, s) for s in range(NH) for t in range(H)]
-        e_now = None
-        late = None
-        for g in range(-1, len(groups)):
-            e_next = None
-            if g + 1 < len(groups):
-                t_next, s_next = groups[g + 1]
-                project_q(t_next, s_next)
-                if s_next == 0:
-                    for s in range(NH):
-                        project_k(t_next, s)
-                e_next = probs.tile([P, TB, HALF], BF16, name="e")
-            for j in range(QB):
-                if g < 0:
-                    project_v(2 * j)
-                    project_v(2 * j + 1)
-                else:
-                    o_tok = attend(groups[g][0], j, e_now)
-                if e_next is not None:
-                    exp_scores(t_next, s_next, 2 * j, e_next)
-                    exp_scores(t_next, s_next, 2 * j + 1, e_next)
-                if late is not None:
-                    flip_back(*late)
-                if g >= 0:
-                    if j == 0:
-                        flip_ps = flip.tile([P, HALF], BF16, name="flip_ps", tag="flip")
-                    late = (o_tok, groups[g][0], groups[g][1], j, flip_ps)
+        last = len(groups) - 1
+
+        def between_rounds(g):
+            if g + 2 < H:
+                project_q(g + 2, 0)
+                project_k(g + 2, 0)
+                project_k(g + 2, 1)
+            if H <= g + 3 <= last:
+                project_q(g + 3 - H, 1)
             if g >= H:
                 project_out(g - H, 0)
+
+        project_q(0, 0)
+        project_k(0, 0)
+        for i in range(QB):
+            project_v(i)
+        project_k(0, 1)
+        e_next = probs.tile([P, TB, HALF], BF16, name="e")
+        for i in range(TB):
+            exp_scores(0, 0, i, e_next)
+            if QB + i < TB:
+                project_v(QB + i)
+        between_rounds(-1)
+
+        late = None
+        for g, (t, s) in enumerate(groups):
             e_now = e_next
+            if g < last:
+                t_next, s_next = groups[g + 1]
+                e_next = probs.tile([P, TB, HALF], BF16, name="e")
+            for j in range(QB):
+                if g < last:
+                    for i in range(KEYS_A_STEP * j, KEYS_A_STEP * (j + 1)):
+                        exp_scores(t_next, s_next, i, e_next)
+                o_tok = attend(t, j, e_now)
+                if late is not None:
+                    flip_back(*late)
+                if j == 0:
+                    flip_ps = flip.tile([P, HALF], BF16, name="flip_ps", tag="flip")
+                late = (o_tok, t, s, j, flip_ps)
+            between_rounds(g)
         flip_back(*late)
         for m in range(CB):
             project_out(m, 1)

@@ -18,6 +18,7 @@ NH = N // HALF
 TB = N // P
 QB = HALF // P
 KEYS_A_STEP = TB // QB
+S_SCALAR = 640
 FLOPS = 2 * (4 * C * C * N + 2 * H * N * N * DH)
 
 
@@ -29,20 +30,33 @@ def tile_transformerencoder_b_kernel(
         tc.tile_pool(name="lists", bufs=1) as lists,
         tc.tile_pool(name="held", bufs=1) as held,
         tc.tile_pool(name="work", bufs=3) as work,
+        tc.tile_pool(name="squares", bufs=CB) as squares,
+        tc.tile_pool(name="stores", bufs=CB) as stores,
         tc.tile_pool(name="probs", bufs=2) as probs,
         tc.psum_pool(name="banks", bufs=5) as banks,
         tc.psum_pool(name="ctx", bufs=2) as ctx,
         tc.psum_pool(name="flip", bufs=1) as flip,
     ):
+        def cols(s):
+            return slice(s * HALF, (s + 1) * HALF)
+
         offsets = lists.tile([P, N // 16], U16, name="offsets")
         nc.sync.dma_start(offsets[:], offs)
 
         table = [held.tile([P, S], F32, name=f"table{b}") for b in range(CB)]
         pos_sb = [held.tile([P, N], F32, name=f"pos{b}") for b in range(CB)]
+        weights = {name: held.tile([P, CB, C], BF16, name=f"w{name}") for name in "qkvo"}
+        bv_row = held.tile([P, C], F32, name="bv_row")
+
+        def load_pos(b, s):
+            nc.sync.dma_start(pos_sb[b][:, cols(s)], pos[b * P : (b + 1) * P, cols(s)])
+
+        def load_weights(name, w):
+            nc.sync.dma_start(weights[name][:], w.rearrange("(b p) m -> p b m", p=P))
+
         for b in range(CB):
             nc.sync.dma_start(table[b][:], emb[b * P : (b + 1) * P, :])
-            nc.sync.dma_start(pos_sb[b][:], pos[b * P : (b + 1) * P, :])
-
+            load_pos(b, 0)
         per_channel = {}
         with nc.allow_non_contiguous_dma(reason="512 floats, one to a partition"):
             for name, vec in (("ln_w", ln_w), ("ln_b", ln_b), ("bq", bq), ("bo", bo)):
@@ -50,13 +64,13 @@ def tile_transformerencoder_b_kernel(
                 nc.sync.dma_start(
                     per_channel[name][:], vec.rearrange("(b p) o -> p (b o)", p=P)
                 )
-        bv_row = held.tile([P, C], F32, name="bv_row")
+        load_weights("q", wq)
+        load_weights("k", wk)
+        load_weights("v", wv)
         nc.sync.dma_start(bv_row[:], bv.rearrange("c o -> (c o)").partition_broadcast(P))
-
-        weights = {}
-        for name, w in (("q", wq), ("k", wk), ("v", wv), ("o", wo)):
-            weights[name] = held.tile([P, CB, C], BF16, name=f"w{name}")
-            nc.sync.dma_start(weights[name][:], w.rearrange("(b p) m -> p b m", p=P))
+        for b in range(CB):
+            load_pos(b, 1)
+        load_weights("o", wo)
 
         mean_w = held.tile([P, P], F32, name="mean_w")
         nc.vector.memset(mean_w[:], 1.0 / C)
@@ -69,44 +83,63 @@ def tile_transformerencoder_b_kernel(
             nc.gpsimd.memset(v_aug[i][:], 1.0)
 
         x0 = [held.tile([P, N], F32, name=f"x0_{b}") for b in range(CB)]
-        mu_ps = [banks.tile([P, HALF], F32, name=f"mu_ps{s}", tag="bank") for s in range(NH)]
-        for b in range(CB):
-            nc.scalar.mul(table[b][:, 0 : S // 2], table[b][:, 0 : S // 2], math.sqrt(C))
-            nc.vector.tensor_scalar_mul(table[b][:, S // 2 : S], table[b][:, S // 2 : S], math.sqrt(C))
-            for s in range(NH):
-                cols = slice(s * HALF, (s + 1) * HALF)
-                piece = offsets[:, s * HALF // 16 : (s + 1) * HALF // 16]
-                nc.vector.tensor_tensor(
-                    x0[b][:, cols], table[b][:].indirect(piece), pos_sb[b][:, cols], ALU.add
-                )
-                nc.tensor.matmul(
-                    mu_ps[s][:], mean_w[:], x0[b][:, cols], start=(b == 0), stop=(b == CB - 1)
-                )
-
         xc = [held.tile([P, N], F32, name=f"xc{b}") for b in range(CB)]
         rstd = held.tile([P, N], F32, name="rstd")
         h = [held.tile([P, N], BF16, name=f"h{b}") for b in range(CB)]
-        var_ps = [banks.tile([P, HALF], F32, name=f"var_ps{s}", tag="bank") for s in range(NH)]
-        for s in range(NH):
-            cols = slice(s * HALF, (s + 1) * HALF)
+
+        def mean_over_channels(ps, parts, b, total):
+            if total is None:
+                nc.tensor.matmul(ps[:], mean_w[:], parts[b], start=(b == 0), stop=(b == CB - 1))
+                return
+            if b > 0:
+                nc.vector.tensor_tensor(
+                    total[:], parts[0] if b == 1 else total[:], parts[b], ALU.add
+                )
+            if b == CB - 1:
+                nc.tensor.matmul(ps[:], mean_w[:], total[:], start=True, stop=True)
+
+        def look_up_and_sum(s, summed):
+            mu_ps = ctx.tile([P, HALF], F32, name="mu_ps", tag="ctx")
+            m2_ps = ctx.tile([P, HALF], F32, name="m2_ps", tag="ctx")
+            sum_x = work.tile([P, HALF], F32, name="sum_x") if summed else None
+            sum_sq = work.tile([P, HALF], F32, name="sum_sq") if summed else None
+            piece = offsets[:, s * HALF // 16 : (s + 1) * HALF // 16]
+            sqs = []
             for b in range(CB):
-                nc.vector.tensor_tensor(xc[b][:, cols], x0[b][:, cols], mu_ps[s][:], ALU.subtract)
-                sq = work.tile([P, HALF], F32, name="sq")
-                nc.scalar.activation(sq[:], xc[b][:, cols], ACT.Square)
-                nc.tensor.matmul(var_ps[s][:], mean_w[:], sq[:], start=(b == 0), stop=(b == CB - 1))
-        for s in range(NH):
-            cols = slice(s * HALF, (s + 1) * HALF)
-            nc.scalar.activation(rstd[:, cols], var_ps[s][:], ACT.Abs_reciprocal_sqrt, bias=eps[:])
+                nc.vector.tensor_tensor(
+                    x0[b][:, cols(s)], table[b][:].indirect(piece), pos_sb[b][:, cols(s)], ALU.add
+                )
+                sq = squares.tile([P, HALF], F32, name="sq")
+                nc.scalar.activation(sq[:], x0[b][:, cols(s)], ACT.Square)
+                sqs.append(sq[:])
+                mean_over_channels(mu_ps, [x[:, cols(s)] for x in x0], b, sum_x)
+                mean_over_channels(m2_ps, sqs, b, sum_sq)
+            return mu_ps, m2_ps
+
+        def normalise(s, mu_ps, m2_ps):
+            mu_sq = work.tile([P, HALF], F32, name="mu_sq")
+            nc.scalar.activation(mu_sq[:], mu_ps[:], ACT.Square)
+            var = work.tile([P, HALF], F32, name="var")
+            nc.vector.tensor_tensor(var[:], m2_ps[:], mu_sq[:], ALU.subtract)
+            nc.scalar.activation(rstd[:, cols(s)], var[:], ACT.Abs_reciprocal_sqrt, bias=eps[:])
+            for b in range(CB):
+                nc.vector.tensor_tensor(xc[b][:, cols(s)], x0[b][:, cols(s)], mu_ps[:], ALU.subtract)
             for b in range(CB):
                 xn = work.tile([P, HALF], F32, name="xn")
-                nc.vector.tensor_tensor(xn[:], xc[b][:, cols], rstd[:, cols], ALU.mult)
+                nc.vector.tensor_tensor(xn[:], xc[b][:, cols(s)], rstd[:, cols(s)], ALU.mult)
                 nc.scalar.activation(
-                    h[b][:, cols],
+                    h[b][:, cols(s)],
                     xn[:],
                     ACT.Identity,
                     bias=per_channel["ln_b"][:, b : b + 1],
                     scale=per_channel["ln_w"][:, b : b + 1],
                 )
+
+        for b in range(CB):
+            nc.scalar.mul(table[b][:, 0:S_SCALAR], table[b][:, 0:S_SCALAR], math.sqrt(C))
+            nc.vector.tensor_scalar_mul(table[b][:, S_SCALAR:S], table[b][:, S_SCALAR:S], math.sqrt(C))
+        normalise(0, *look_up_and_sum(0, summed=False))
+        normalise(1, *look_up_and_sum(1, summed=True))
 
         q = [held.tile([P, N], BF16, name=f"q{t}") for t in range(H)]
         k = [held.tile([P, N], BF16, name=f"k{t}") for t in range(H)]
@@ -118,7 +151,7 @@ def tile_transformerencoder_b_kernel(
                 nc.tensor.matmul(
                     ps[:],
                     w[:, b, t * DH : (t + 1) * DH],
-                    h[b][:, s * HALF : (s + 1) * HALF],
+                    h[b][:, cols(s)],
                     start=(b == 0),
                     stop=(b == CB - 1),
                 )
@@ -126,13 +159,18 @@ def tile_transformerencoder_b_kernel(
 
         def project_k(t, s):
             ps = project(weights["k"], t, s)
-            nc.vector.tensor_copy(k[t][:, s * HALF : (s + 1) * HALF], ps[:])
+            if s == 0:
+                nc.scalar.copy(k[t][:, cols(s)], ps[:])
+            else:
+                nc.vector.tensor_copy(k[t][:, cols(s)], ps[:])
 
         def project_q(t, s):
             ps = project(weights["q"], t, s)
-            nc.vector.tensor_scalar_add(
-                q[t][:, s * HALF : (s + 1) * HALF], ps[:], per_channel["bq"][:, t : t + 1]
-            )
+            bias = per_channel["bq"][:, t : t + 1]
+            if s == 0:
+                nc.scalar.activation(q[t][:, cols(s)], ps[:], ACT.Identity, bias=bias)
+            else:
+                nc.vector.tensor_scalar_add(q[t][:, cols(s)], ps[:], bias)
 
         def project_v(i):
             ps = banks.tile([P, C], F32, name="v_ps", tag="bank")
@@ -154,11 +192,7 @@ def tile_transformerencoder_b_kernel(
         def exp_scores(t, s, i, e):
             ps = banks.tile([P, HALF], F32, name="sc_ps", tag="bank")
             nc.tensor.matmul(
-                ps[:],
-                k[t][:, i * P : (i + 1) * P],
-                q[t][:, s * HALF : (s + 1) * HALF],
-                start=True,
-                stop=True,
+                ps[:], k[t][:, i * P : (i + 1) * P], q[t][:, cols(s)], start=True, stop=True
             )
             nc.scalar.activation(e[:, i, :], ps[:], ACT.Exp, scale=1.0 / math.sqrt(DH))
 
@@ -181,40 +215,38 @@ def tile_transformerencoder_b_kernel(
         def flip_back(o_tok, t, s, j, flip_ps):
             nc.tensor.transpose(flip_ps[:, j * P : (j + 1) * P], o_tok[:], ident[:])
             if j == QB - 1:
-                nc.vector.tensor_copy(o[t][:, s * HALF : (s + 1) * HALF], flip_ps[:])
+                nc.vector.tensor_copy(o[t][:, cols(s)], flip_ps[:])
 
         def project_out(m, s):
-            cols = slice(s * HALF, (s + 1) * HALF)
             ps = banks.tile([P, HALF], F32, name="y_ps", tag="bank")
             for t in range(H):
                 nc.tensor.matmul(
                     ps[:],
                     weights["o"][:, t, m * P : (m + 1) * P],
-                    o[t][:, cols],
+                    o[t][:, cols(s)],
                     start=(t == 0),
                     stop=(t == H - 1),
                 )
-            y = work.tile([P, HALF], F32, name="y")
+            y = stores.tile([P, HALF], F32, name="y")
             nc.vector.scalar_tensor_tensor(
-                y[:], ps[:], per_channel["bo"][:, m : m + 1], x0[m][:, cols], ALU.add, ALU.add
+                y[:], ps[:], per_channel["bo"][:, m : m + 1], x0[m][:, cols(s)], ALU.add, ALU.add
             )
-            nc.sync.dma_start(out[m * P : (m + 1) * P, cols], y[:])
+            nc.sync.dma_start(out[m * P : (m + 1) * P, cols(s)], y[:])
 
         groups = [(t, s) for s in range(NH) for t in range(H)]
         last = len(groups) - 1
 
         def between_rounds(g):
             if g + 2 < H:
-                project_q(g + 2, 0)
-                project_k(g + 2, 0)
                 project_k(g + 2, 1)
             if H <= g + 3 <= last:
                 project_q(g + 3 - H, 1)
             if g >= H:
                 project_out(g - H, 0)
 
-        project_q(0, 0)
-        project_k(0, 0)
+        for t in range(H):
+            project_q(t, 0)
+            project_k(t, 0)
         for i in range(QB):
             project_v(i)
         project_k(0, 1)

@@ -57,6 +57,7 @@ def tile_transformerencoder_b_kernel(
         for b in range(CB):
             nc.sync.dma_start(table[b][:], emb[b * P : (b + 1) * P, :])
             load_pos(b, 0)
+        load_pos(0, 1)
         per_channel = {}
         with nc.allow_non_contiguous_dma(reason="512 floats, one to a partition"):
             for name, vec in (("ln_w", ln_w), ("ln_b", ln_b), ("bq", bq), ("bo", bo)):
@@ -68,7 +69,7 @@ def tile_transformerencoder_b_kernel(
         load_weights("k", wk)
         load_weights("v", wv)
         nc.sync.dma_start(bv_row[:], bv.rearrange("c o -> (c o)").partition_broadcast(P))
-        for b in range(CB):
+        for b in range(1, CB):
             load_pos(b, 1)
         load_weights("o", wo)
 
@@ -87,22 +88,22 @@ def tile_transformerencoder_b_kernel(
         rstd = held.tile([P, N], F32, name="rstd")
         h = [held.tile([P, N], BF16, name=f"h{b}") for b in range(CB)]
 
-        def mean_over_channels(ps, parts, b, total):
-            if total is None:
+        def mean_over_channels(ps, parts, b, direct, total):
+            if b < direct:
                 nc.tensor.matmul(ps[:], mean_w[:], parts[b], start=(b == 0), stop=(b == CB - 1))
                 return
-            if b > 0:
+            if b > direct:
                 nc.vector.tensor_tensor(
-                    total[:], parts[0] if b == 1 else total[:], parts[b], ALU.add
+                    total[:], parts[direct] if b == direct + 1 else total[:], parts[b], ALU.add
                 )
             if b == CB - 1:
-                nc.tensor.matmul(ps[:], mean_w[:], total[:], start=True, stop=True)
+                nc.tensor.matmul(ps[:], mean_w[:], total[:], start=(direct == 0), stop=True)
 
-        def look_up_and_sum(s, summed):
+        def look_up_and_sum(s, direct):
             mu_ps = ctx.tile([P, HALF], F32, name="mu_ps", tag="ctx")
             m2_ps = ctx.tile([P, HALF], F32, name="m2_ps", tag="ctx")
-            sum_x = work.tile([P, HALF], F32, name="sum_x") if summed else None
-            sum_sq = work.tile([P, HALF], F32, name="sum_sq") if summed else None
+            sum_x = work.tile([P, HALF], F32, name="sum_x") if direct < CB else None
+            sum_sq = work.tile([P, HALF], F32, name="sum_sq") if direct < CB else None
             piece = offsets[:, s * HALF // 16 : (s + 1) * HALF // 16]
             sqs = []
             for b in range(CB):
@@ -112,8 +113,8 @@ def tile_transformerencoder_b_kernel(
                 sq = squares.tile([P, HALF], F32, name="sq")
                 nc.scalar.activation(sq[:], x0[b][:, cols(s)], ACT.Square)
                 sqs.append(sq[:])
-                mean_over_channels(mu_ps, [x[:, cols(s)] for x in x0], b, sum_x)
-                mean_over_channels(m2_ps, sqs, b, sum_sq)
+                mean_over_channels(mu_ps, [x[:, cols(s)] for x in x0], b, direct, sum_x)
+                mean_over_channels(m2_ps, sqs, b, direct, sum_sq)
             return mu_ps, m2_ps
 
         def normalise(s, mu_ps, m2_ps):
@@ -138,8 +139,8 @@ def tile_transformerencoder_b_kernel(
         for b in range(CB):
             nc.scalar.mul(table[b][:, 0:S_SCALAR], table[b][:, 0:S_SCALAR], math.sqrt(C))
             nc.vector.tensor_scalar_mul(table[b][:, S_SCALAR:S], table[b][:, S_SCALAR:S], math.sqrt(C))
-        normalise(0, *look_up_and_sum(0, summed=False))
-        normalise(1, *look_up_and_sum(1, summed=True))
+        normalise(0, *look_up_and_sum(0, direct=CB))
+        normalise(1, *look_up_and_sum(1, direct=1))
 
         q = [held.tile([P, N], BF16, name=f"q{t}") for t in range(H)]
         k = [held.tile([P, N], BF16, name=f"k{t}") for t in range(H)]

@@ -31,7 +31,7 @@ def tile_transformerencoder_b_kernel(
         tc.tile_pool(name="held", bufs=1) as held,
         tc.tile_pool(name="work", bufs=3) as work,
         tc.tile_pool(name="squares", bufs=CB) as squares,
-        tc.tile_pool(name="stores", bufs=CB) as stores,
+        tc.tile_pool(name="stores", bufs=CB + 1) as stores,
         tc.tile_pool(name="probs", bufs=2) as probs,
         tc.psum_pool(name="banks", bufs=5) as banks,
         tc.psum_pool(name="ctx", bufs=2) as ctx,
@@ -218,21 +218,22 @@ def tile_transformerencoder_b_kernel(
             if j == QB - 1:
                 nc.vector.tensor_copy(o[t][:, cols(s)], flip_ps[:])
 
-        def project_out(m, s):
-            ps = banks.tile([P, HALF], F32, name="y_ps", tag="bank")
+        def project_out(m, tokens):
+            width = tokens.stop - tokens.start
+            ps = banks.tile([P, width], F32, name="y_ps", tag="bank")
             for t in range(H):
                 nc.tensor.matmul(
                     ps[:],
                     weights["o"][:, t, m * P : (m + 1) * P],
-                    o[t][:, cols(s)],
+                    o[t][:, tokens],
                     start=(t == 0),
                     stop=(t == H - 1),
                 )
-            y = stores.tile([P, HALF], F32, name="y")
+            y = stores.tile([P, width], F32, name="y")
             nc.vector.scalar_tensor_tensor(
-                y[:], ps[:], per_channel["bo"][:, m : m + 1], x0[m][:, cols(s)], ALU.add, ALU.add
+                y[:], ps[:], per_channel["bo"][:, m : m + 1], x0[m][:, tokens], ALU.add, ALU.add
             )
-            nc.sync.dma_start(out[m * P : (m + 1) * P, cols(s)], y[:])
+            nc.sync.dma_start(out[m * P : (m + 1) * P, tokens], y[:])
 
         groups = [(t, s) for s in range(NH) for t in range(H)]
         last = len(groups) - 1
@@ -243,7 +244,7 @@ def tile_transformerencoder_b_kernel(
             if H <= g + 3 <= last:
                 project_q(g + 3 - H, 1)
             if g >= H:
-                project_out(g - H, 0)
+                project_out(g - H, cols(0))
 
         for t in range(H):
             project_q(t, 0)
@@ -276,5 +277,7 @@ def tile_transformerencoder_b_kernel(
                 late = (o_tok, t, s, j, flip_ps)
             between_rounds(g)
         flip_back(*late)
-        for m in range(CB):
-            project_out(m, 1)
+        for m in range(CB - 1):
+            project_out(m, cols(1))
+        project_out(CB - 1, slice(HALF, HALF + HALF // 2))
+        project_out(CB - 1, slice(HALF + HALF // 2, N))

@@ -14,7 +14,10 @@ C, S, N, H, DH = 512, 2048, 1024, 4, 128
 EPS = 1e-5
 CB = C // P
 HALF = 512
+ROWS = 32
 NH = N // HALF
+WIDTH = HALF // 2
+PIECES = [slice(j, j + WIDTH) for j in range(0, N, WIDTH)]
 TB = N // P
 QB = HALF // P
 KEYS_A_STEP = TB // QB
@@ -48,44 +51,52 @@ def tile_transformerencoder_b_kernel(
         weights = {name: held.tile([P, CB, C], BF16, name=f"w{name}") for name in "qkvo"}
         bv_row = held.tile([P, C], F32, name="bv_row")
 
-        def load_pos(b, s):
-            nc.sync.dma_start(pos_sb[b][:, cols(s)], pos[b * P : (b + 1) * P, cols(s)])
+        def load_pos(b, piece):
+            nc.sync.dma_start(pos_sb[b][:, piece], pos[b * P : (b + 1) * P, piece])
 
         def load_weights(name, w):
             nc.sync.dma_start(weights[name][:], w.rearrange("(b p) m -> p b m", p=P))
 
+        rows = held.tile([ROWS, P], F32, name="rows")
+        nc.vector.memset(rows[:], 0.0)
+        vectors = {"ln_w": ln_w, "ln_b": ln_b, "bq": bq, "bo": bo}
+        for n, vec in enumerate(vectors.values()):
+            nc.sync.dma_start(
+                rows[CB * n : CB * (n + 1), :], vec.rearrange("(b p) o -> b (p o)", p=P)
+            )
         for b in range(CB):
             nc.sync.dma_start(table[b][:], emb[b * P : (b + 1) * P, :])
-            load_pos(b, 0)
-        load_pos(0, 1)
-        per_channel = {}
-        with nc.allow_non_contiguous_dma(reason="512 floats, one to a partition"):
-            for name, vec in (("ln_w", ln_w), ("ln_b", ln_b), ("bq", bq), ("bo", bo)):
-                per_channel[name] = held.tile([P, CB], F32, name=name)
-                nc.sync.dma_start(
-                    per_channel[name][:], vec.rearrange("(b p) o -> p (b o)", p=P)
-                )
+            load_pos(b, cols(0))
         load_weights("q", wq)
         load_weights("k", wk)
+        for b in range(CB):
+            load_pos(b, cols(1))
         load_weights("v", wv)
         nc.sync.dma_start(bv_row[:], bv.rearrange("c o -> (c o)").partition_broadcast(P))
-        for b in range(1, CB):
-            load_pos(b, 1)
         load_weights("o", wo)
 
         mean_w = held.tile([P, P], F32, name="mean_w")
         nc.vector.memset(mean_w[:], 1.0 / C)
         eps = held.tile([P, 1], F32, name="eps")
         nc.vector.memset(eps[:], EPS)
+        first = held.tile([P, 1], F32, name="first")
+        nc.scalar.activation(first[:], eps[:], ACT.Abs_reciprocal_sqrt)
         ident = held.tile([P, P], BF16, name="ident")
         make_identity(nc, ident[:])
+        ident_f = held.tile([ROWS, ROWS], F32, name="ident_f")
+        make_identity(nc, ident_f[:])
+        columns_ps = banks.tile([P, ROWS], F32, name="columns_ps", tag="bank")
+        nc.tensor.matmul(columns_ps[:], rows[:], ident_f[:])
+        columns = held.tile([P, ROWS], F32, name="columns")
+        nc.vector.tensor_copy(columns[:], columns_ps[:])
+        per_channel = {
+            name: columns[:, CB * n : CB * (n + 1)] for n, name in enumerate(vectors)
+        }
         v_aug = [held.tile([P, H, DH + 1], BF16, name=f"v_aug{i}") for i in range(TB)]
         for i in range(TB):
             nc.gpsimd.memset(v_aug[i][:], 1.0)
 
-        x0 = [held.tile([P, N], F32, name=f"x0_{b}") for b in range(CB)]
-        xc = [held.tile([P, N], F32, name=f"xc{b}") for b in range(CB)]
-        rstd = held.tile([P, N], F32, name="rstd")
+        x0 = held.tile([P, CB, N], F32, name="x0")
         h = [held.tile([P, N], BF16, name=f"h{b}") for b in range(CB)]
 
         def mean_over_channels(ps, parts, b, direct, total):
@@ -99,37 +110,41 @@ def tile_transformerencoder_b_kernel(
             if b == CB - 1:
                 nc.tensor.matmul(ps[:], mean_w[:], total[:], start=(direct == 0), stop=True)
 
-        def look_up_and_sum(s, direct):
-            mu_ps = ctx.tile([P, HALF], F32, name="mu_ps", tag="ctx")
-            m2_ps = ctx.tile([P, HALF], F32, name="m2_ps", tag="ctx")
-            sum_x = work.tile([P, HALF], F32, name="sum_x") if direct < CB else None
-            sum_sq = work.tile([P, HALF], F32, name="sum_sq") if direct < CB else None
-            piece = offsets[:, s * HALF // 16 : (s + 1) * HALF // 16]
+        def look_up_and_sum(piece, direct, pool, tag):
+            width = piece.stop - piece.start
+            mu_ps = pool.tile([P, width], F32, name="mu_ps", tag=tag)
+            m2_ps = pool.tile([P, width], F32, name="m2_ps", tag=tag)
+            sum_x = work.tile([P, width], F32, name="sum_x") if direct < CB else None
+            sum_sq = work.tile([P, width], F32, name="sum_sq") if direct < CB else None
+            words = offsets[:, piece.start // 16 : piece.stop // 16]
             sqs = []
             for b in range(CB):
                 nc.vector.tensor_tensor(
-                    x0[b][:, cols(s)], table[b][:].indirect(piece), pos_sb[b][:, cols(s)], ALU.add
+                    x0[:, b, piece], table[b][:].indirect(words), pos_sb[b][:, piece], ALU.add
                 )
-                sq = squares.tile([P, HALF], F32, name="sq")
-                nc.scalar.activation(sq[:], x0[b][:, cols(s)], ACT.Square)
+                sq = squares.tile([P, width], F32, name="sq")
+                nc.scalar.activation(sq[:], x0[:, b, piece], ACT.Square)
                 sqs.append(sq[:])
-                mean_over_channels(mu_ps, [x[:, cols(s)] for x in x0], b, direct, sum_x)
+                mean_over_channels(mu_ps, [x0[:, c, piece] for c in range(CB)], b, direct, sum_x)
                 mean_over_channels(m2_ps, sqs, b, direct, sum_sq)
             return mu_ps, m2_ps
 
-        def normalise(s, mu_ps, m2_ps):
-            mu_sq = work.tile([P, HALF], F32, name="mu_sq")
+        def normalise(piece, mu_ps, m2_ps):
+            width = piece.stop - piece.start
+            mu_sq = work.tile([P, width], F32, name="mu_sq")
             nc.scalar.activation(mu_sq[:], mu_ps[:], ACT.Square)
-            var = work.tile([P, HALF], F32, name="var")
+            var = work.tile([P, width], F32, name="var")
             nc.vector.tensor_tensor(var[:], m2_ps[:], mu_sq[:], ALU.subtract)
-            nc.scalar.activation(rstd[:, cols(s)], var[:], ACT.Abs_reciprocal_sqrt, bias=eps[:])
+            rstd = work.tile([P, width], F32, name="rstd")
+            nc.scalar.activation(rstd[:], var[:], ACT.Abs_reciprocal_sqrt, bias=eps[:])
+            xc = work.tile([P, CB, width], F32, name="xc", bufs=2)
             for b in range(CB):
-                nc.vector.tensor_tensor(xc[b][:, cols(s)], x0[b][:, cols(s)], mu_ps[:], ALU.subtract)
+                nc.vector.tensor_tensor(xc[:, b, :], x0[:, b, piece], mu_ps[:], ALU.subtract)
             for b in range(CB):
-                xn = work.tile([P, HALF], F32, name="xn")
-                nc.vector.tensor_tensor(xn[:], xc[b][:, cols(s)], rstd[:, cols(s)], ALU.mult)
+                xn = work.tile([P, width], F32, name="xn")
+                nc.vector.tensor_tensor(xn[:], xc[:, b, :], rstd[:], ALU.mult)
                 nc.scalar.activation(
-                    h[b][:, cols(s)],
+                    h[b][:, piece],
                     xn[:],
                     ACT.Identity,
                     bias=per_channel["ln_b"][:, b : b + 1],
@@ -139,39 +154,41 @@ def tile_transformerencoder_b_kernel(
         for b in range(CB):
             nc.scalar.mul(table[b][:, 0:S_SCALAR], table[b][:, 0:S_SCALAR], math.sqrt(C))
             nc.vector.tensor_scalar_mul(table[b][:, S_SCALAR:S], table[b][:, S_SCALAR:S], math.sqrt(C))
-        normalise(0, *look_up_and_sum(0, direct=CB))
-        normalise(1, *look_up_and_sum(1, direct=1))
+        normalise(PIECES[0], *look_up_and_sum(PIECES[0], CB, ctx, "ctx"))
+        normalise(PIECES[1], *look_up_and_sum(PIECES[1], CB, banks, "bank"))
+        for piece in PIECES[2:]:
+            normalise(piece, *look_up_and_sum(piece, 0, ctx, "ctx"))
 
         q = [held.tile([P, N], BF16, name=f"q{t}") for t in range(H)]
         k = [held.tile([P, N], BF16, name=f"k{t}") for t in range(H)]
         o = [held.tile([P, N], BF16, name=f"o{t}") for t in range(H)]
 
-        def project(w, t, s):
-            ps = banks.tile([P, HALF], F32, name="proj_ps", tag="bank")
+        def project(w, t, piece):
+            ps = banks.tile([P, piece.stop - piece.start], F32, name="proj_ps", tag="bank")
             for b in range(CB):
                 nc.tensor.matmul(
                     ps[:],
                     w[:, b, t * DH : (t + 1) * DH],
-                    h[b][:, cols(s)],
+                    h[b][:, piece],
                     start=(b == 0),
                     stop=(b == CB - 1),
                 )
             return ps
 
-        def project_k(t, s):
-            ps = project(weights["k"], t, s)
-            if s == 0:
-                nc.scalar.copy(k[t][:, cols(s)], ps[:])
+        def project_k(t, piece):
+            ps = project(weights["k"], t, piece)
+            if piece.stop < N:
+                nc.scalar.copy(k[t][:, piece], ps[:])
             else:
-                nc.vector.tensor_copy(k[t][:, cols(s)], ps[:])
+                nc.vector.tensor_copy(k[t][:, piece], ps[:])
 
-        def project_q(t, s):
-            ps = project(weights["q"], t, s)
+        def project_q(t, piece):
+            ps = project(weights["q"], t, piece)
             bias = per_channel["bq"][:, t : t + 1]
-            if s == 0:
-                nc.scalar.activation(q[t][:, cols(s)], ps[:], ACT.Identity, bias=bias)
+            if piece.stop < N:
+                nc.scalar.activation(q[t][:, piece], ps[:], ACT.Identity, bias=bias)
             else:
-                nc.vector.tensor_scalar_add(q[t][:, cols(s)], ps[:], bias)
+                nc.vector.tensor_scalar_add(q[t][:, piece], ps[:], bias)
 
         def project_v(i):
             ps = banks.tile([P, C], F32, name="v_ps", tag="bank")
@@ -231,7 +248,7 @@ def tile_transformerencoder_b_kernel(
                 )
             y = stores.tile([P, width], F32, name="y")
             nc.vector.scalar_tensor_tensor(
-                y[:], ps[:], per_channel["bo"][:, m : m + 1], x0[m][:, tokens], ALU.add, ALU.add
+                y[:], ps[:], per_channel["bo"][:, m : m + 1], x0[:, m, tokens], ALU.add, ALU.add
             )
             nc.sync.dma_start(out[m * P : (m + 1) * P, tokens], y[:])
 
@@ -239,25 +256,30 @@ def tile_transformerencoder_b_kernel(
         last = len(groups) - 1
 
         def between_rounds(g):
-            if g + 2 < H:
-                project_k(g + 2, 1)
-            if H <= g + 3 <= last:
-                project_q(g + 3 - H, 1)
-            if g >= H:
+            if g < H:
+                project_q(g, PIECES[3])
+            else:
                 project_out(g - H, cols(0))
 
+        for piece in PIECES[:2]:
+            for t in range(H):
+                project_q(t, piece)
+                project_k(t, piece)
+            for i in range(piece.start // P, piece.stop // P):
+                project_v(i)
         for t in range(H):
-            project_q(t, 0)
-            project_k(t, 0)
-        for i in range(QB):
-            project_v(i)
-        project_k(0, 1)
+            project_k(t, PIECES[2])
+        for t in range(H):
+            project_q(t, PIECES[2])
         e_next = probs.tile([P, TB, HALF], BF16, name="e")
         for i in range(TB):
             exp_scores(0, 0, i, e_next)
-            if QB + i < TB:
+            if i < 2:
                 project_v(QB + i)
-        between_rounds(-1)
+            elif i < TB - 2:
+                project_k(i - 2, PIECES[3])
+            else:
+                project_v(i)
 
         late = None
         for g, (t, s) in enumerate(groups):

@@ -14,12 +14,13 @@ C, S, N, H, DH = 512, 2048, 1024, 4, 128
 EPS = 1e-5
 CB = C // P
 HALF = 512
-ROWS = 32
 NH = N // HALF
 WIDTH = HALF // 2
 PIECES = [slice(j, j + WIDTH) for j in range(0, N, WIDTH)]
+HEAD_PAIRS = ((0, 1), (2, 3))
 TB = N // P
 QB = HALF // P
+PAIR = 2
 KEYS_A_STEP = TB // QB
 S_SCALAR = 640
 FLOPS = 2 * (4 * C * C * N + 2 * H * N * N * DH)
@@ -51,29 +52,35 @@ def tile_transformerencoder_b_kernel(
         weights = {name: held.tile([P, CB, C], BF16, name=f"w{name}") for name in "qkvo"}
         bv_row = held.tile([P, C], F32, name="bv_row")
 
+        def in_blocks(x):
+            return x.rearrange("(p b) n -> p b n", b=CB)
+
         def load_pos(b, piece):
-            nc.sync.dma_start(pos_sb[b][:, piece], pos[b * P : (b + 1) * P, piece])
+            nc.sync.dma_start(pos_sb[b][:, piece], in_blocks(pos)[:, b, piece])
 
         def load_weights(name, w):
-            nc.sync.dma_start(weights[name][:], w.rearrange("(b p) m -> p b m", p=P))
+            nc.sync.dma_start(weights[name][:], w)
 
-        rows = held.tile([ROWS, P], F32, name="rows")
-        nc.vector.memset(rows[:], 0.0)
-        vectors = {"ln_w": ln_w, "ln_b": ln_b, "bq": bq, "bo": bo}
-        for n, vec in enumerate(vectors.values()):
-            nc.sync.dma_start(
-                rows[CB * n : CB * (n + 1), :], vec.rearrange("(b p) o -> b (p o)", p=P)
-            )
+        def load_vector(name, columns):
+            per_channel[name] = held.tile([P, CB], F32, name=name)
+            with nc.allow_non_contiguous_dma(reason="512 floats, four to a partition"):
+                nc.sync.dma_start(per_channel[name][:], columns)
+
+        per_channel = {}
         for b in range(CB):
-            nc.sync.dma_start(table[b][:], emb[b * P : (b + 1) * P, :])
+            nc.sync.dma_start(table[b][:], in_blocks(emb)[:, b, :])
             load_pos(b, cols(0))
-        load_weights("q", wq)
-        load_weights("k", wk)
+        load_vector("ln_w", ln_w.rearrange("(p b) o -> p (b o)", b=CB))
+        load_vector("ln_b", ln_b.rearrange("(p b) o -> p (b o)", b=CB))
+        load_weights("q", in_blocks(wq))
+        load_weights("k", in_blocks(wk))
+        load_vector("bq", bq.rearrange("(t p) o -> p (t o)", t=H))
         for b in range(CB):
             load_pos(b, cols(1))
-        load_weights("v", wv)
+        load_weights("v", in_blocks(wv))
         nc.sync.dma_start(bv_row[:], bv.rearrange("c o -> (c o)").partition_broadcast(P))
-        load_weights("o", wo)
+        load_weights("o", wo.rearrange("(t p) m -> p t m", t=H))
+        load_vector("bo", bo.rearrange("(p b) o -> p (b o)", b=CB))
 
         mean_w = held.tile([P, P], F32, name="mean_w")
         nc.vector.memset(mean_w[:], 1.0 / C)
@@ -83,15 +90,6 @@ def tile_transformerencoder_b_kernel(
         nc.scalar.activation(first[:], eps[:], ACT.Abs_reciprocal_sqrt)
         ident = held.tile([P, P], BF16, name="ident")
         make_identity(nc, ident[:])
-        ident_f = held.tile([ROWS, ROWS], F32, name="ident_f")
-        make_identity(nc, ident_f[:])
-        columns_ps = banks.tile([P, ROWS], F32, name="columns_ps", tag="bank")
-        nc.tensor.matmul(columns_ps[:], rows[:], ident_f[:])
-        columns = held.tile([P, ROWS], F32, name="columns")
-        nc.vector.tensor_copy(columns[:], columns_ps[:])
-        per_channel = {
-            name: columns[:, CB * n : CB * (n + 1)] for n, name in enumerate(vectors)
-        }
         v_aug = [held.tile([P, H, DH + 1], BF16, name=f"v_aug{i}") for i in range(TB)]
         for i in range(TB):
             nc.gpsimd.memset(v_aug[i][:], 1.0)
@@ -159,36 +157,39 @@ def tile_transformerencoder_b_kernel(
         for piece in PIECES[2:]:
             normalise(piece, *look_up_and_sum(piece, 0, ctx, "ctx"))
 
-        q = [held.tile([P, N], BF16, name=f"q{t}") for t in range(H)]
-        k = [held.tile([P, N], BF16, name=f"k{t}") for t in range(H)]
+        q = held.tile([P, H, N], BF16, name="q")
+        k = held.tile([P, H, N], BF16, name="k")
         o = [held.tile([P, N], BF16, name=f"o{t}") for t in range(H)]
 
-        def project(w, t, piece):
-            ps = banks.tile([P, piece.stop - piece.start], F32, name="proj_ps", tag="bank")
-            for b in range(CB):
-                nc.tensor.matmul(
-                    ps[:],
-                    w[:, b, t * DH : (t + 1) * DH],
-                    h[b][:, piece],
-                    start=(b == 0),
-                    stop=(b == CB - 1),
-                )
+        def project(w, heads, piece):
+            ps = banks.tile([P, len(heads), piece.stop - piece.start], F32, name="proj_ps", tag="bank")
+            for n, t in enumerate(heads):
+                for b in range(CB):
+                    nc.tensor.matmul(
+                        ps[:, n, :],
+                        w[:, b, t * DH : (t + 1) * DH],
+                        h[b][:, piece],
+                        start=(b == 0),
+                        stop=(b == CB - 1),
+                    )
             return ps
 
-        def project_k(t, piece):
-            ps = project(weights["k"], t, piece)
+        def project_k(heads, piece):
+            ps = project(weights["k"], heads, piece)
+            out_k = k[:, heads[0] : heads[-1] + 1, piece]
             if piece.stop < N:
-                nc.scalar.copy(k[t][:, piece], ps[:])
+                nc.scalar.copy(out_k, ps[:])
             else:
-                nc.vector.tensor_copy(k[t][:, piece], ps[:])
+                nc.vector.tensor_copy(out_k, ps[:])
 
-        def project_q(t, piece):
-            ps = project(weights["q"], t, piece)
-            bias = per_channel["bq"][:, t : t + 1]
-            if piece.stop < N:
-                nc.scalar.activation(q[t][:, piece], ps[:], ACT.Identity, bias=bias)
-            else:
-                nc.vector.tensor_scalar_add(q[t][:, piece], ps[:], bias)
+        def project_q(heads, piece):
+            ps = project(weights["q"], heads, piece)
+            for n, t in enumerate(heads):
+                bias = per_channel["bq"][:, t : t + 1]
+                if piece.stop < N:
+                    nc.scalar.activation(q[:, t, piece], ps[:, n, :], ACT.Identity, bias=bias)
+                else:
+                    nc.vector.tensor_scalar_add(q[:, t, piece], ps[:, n, :], bias)
 
         def project_v(i):
             ps = banks.tile([P, C], F32, name="v_ps", tag="bank")
@@ -210,29 +211,34 @@ def tile_transformerencoder_b_kernel(
         def exp_scores(t, s, i, e):
             ps = banks.tile([P, HALF], F32, name="sc_ps", tag="bank")
             nc.tensor.matmul(
-                ps[:], k[t][:, i * P : (i + 1) * P], q[t][:, cols(s)], start=True, stop=True
+                ps[:], k[:, t, i * P : (i + 1) * P], q[:, t, cols(s)], start=True, stop=True
             )
             nc.scalar.activation(e[:, i, :], ps[:], ACT.Exp, scale=1.0 / math.sqrt(DH))
 
-        def attend(t, j, e):
-            ps = ctx.tile([P, DH + 1], F32, name="ctx_ps", tag="ctx")
+        def attend(ps, t, j, e):
             for i in range(TB):
                 nc.tensor.matmul(
-                    ps[:],
+                    ps[:, j % PAIR, :],
                     e[:, i, j * P : (j + 1) * P],
                     v_aug[i][:, t, :],
                     start=(i == 0),
                     stop=(i == TB - 1),
                 )
-            rsum = work.tile([P, 1], F32, name="rsum")
-            nc.vector.reciprocal(rsum[:], ps[:, DH : DH + 1])
-            o_tok = work.tile([P, DH], BF16, name="o_tok")
-            nc.vector.tensor_scalar_mul(o_tok[:], ps[:, 0:DH], rsum[:])
+
+        def divide(ps):
+            rsum = work.tile([P, PAIR, 1], F32, name="rsum")
+            nc.vector.reciprocal(rsum[:], ps[:, :, DH : DH + 1])
+            o_tok = work.tile([P, PAIR, DH], BF16, name="o_tok")
+            nc.vector.tensor_tensor(
+                o_tok[:], ps[:, :, 0:DH], rsum[:].to_broadcast([P, PAIR, DH]), ALU.mult
+            )
             return o_tok
 
-        def flip_back(o_tok, t, s, j, flip_ps):
-            nc.tensor.transpose(flip_ps[:, j * P : (j + 1) * P], o_tok[:], ident[:])
-            if j == QB - 1:
+        def flip_back(o_tok, t, s, first, flip_ps):
+            for n in range(PAIR):
+                j = first + n
+                nc.tensor.transpose(flip_ps[:, j * P : (j + 1) * P], o_tok[:, n, :], ident[:])
+            if first + PAIR == QB:
                 nc.vector.tensor_copy(o[t][:, cols(s)], flip_ps[:])
 
         def project_out(m, tokens):
@@ -241,7 +247,7 @@ def tile_transformerencoder_b_kernel(
             for t in range(H):
                 nc.tensor.matmul(
                     ps[:],
-                    weights["o"][:, t, m * P : (m + 1) * P],
+                    weights["o"][:, t, m::CB],
                     o[t][:, tokens],
                     start=(t == 0),
                     stop=(t == H - 1),
@@ -250,36 +256,36 @@ def tile_transformerencoder_b_kernel(
             nc.vector.scalar_tensor_tensor(
                 y[:], ps[:], per_channel["bo"][:, m : m + 1], x0[:, m, tokens], ALU.add, ALU.add
             )
-            nc.sync.dma_start(out[m * P : (m + 1) * P, tokens], y[:])
+            nc.sync.dma_start(in_blocks(out)[:, m, tokens], y[:])
 
         groups = [(t, s) for s in range(NH) for t in range(H)]
         last = len(groups) - 1
 
         def between_rounds(g):
-            if g < H:
-                project_q(g, PIECES[3])
-            else:
+            if g in (0, 2):
+                project_q(HEAD_PAIRS[g // 2], PIECES[3])
+            if g >= H:
                 project_out(g - H, cols(0))
 
         for piece in PIECES[:2]:
-            for t in range(H):
-                project_q(t, piece)
-                project_k(t, piece)
+            for heads in HEAD_PAIRS:
+                project_q(heads, piece)
+                project_k(heads, piece)
             for i in range(piece.start // P, piece.stop // P):
                 project_v(i)
-        for t in range(H):
-            project_k(t, PIECES[2])
-        for t in range(H):
-            project_q(t, PIECES[2])
+        for heads in HEAD_PAIRS:
+            project_k(heads, PIECES[2])
+        for heads in HEAD_PAIRS:
+            project_q(heads, PIECES[2])
         e_next = probs.tile([P, TB, HALF], BF16, name="e")
         for i in range(TB):
             exp_scores(0, 0, i, e_next)
             if i < 2:
                 project_v(QB + i)
-            elif i < TB - 2:
-                project_k(i - 2, PIECES[3])
-            else:
-                project_v(i)
+            elif i < 4:
+                project_k(HEAD_PAIRS[i - 2], PIECES[3])
+            elif i < 6:
+                project_v(QB + i - 2)
 
         late = None
         for g, (t, s) in enumerate(groups):
@@ -291,12 +297,15 @@ def tile_transformerencoder_b_kernel(
                 if g < last:
                     for i in range(KEYS_A_STEP * j, KEYS_A_STEP * (j + 1)):
                         exp_scores(t_next, s_next, i, e_next)
-                o_tok = attend(t, j, e_now)
-                if late is not None:
-                    flip_back(*late)
-                if j == 0:
-                    flip_ps = flip.tile([P, HALF], BF16, name="flip_ps", tag="flip")
-                late = (o_tok, t, s, j, flip_ps)
+                if j % PAIR == 0:
+                    ps = ctx.tile([P, PAIR, DH + 1], F32, name="ctx_ps", tag="ctx")
+                attend(ps, t, j, e_now)
+                if j % PAIR == PAIR - 1:
+                    if late is not None:
+                        flip_back(*late)
+                    if j == PAIR - 1:
+                        flip_ps = flip.tile([P, HALF], BF16, name="flip_ps", tag="flip")
+                    late = (divide(ps), t, s, j + 1 - PAIR, flip_ps)
             between_rounds(g)
         flip_back(*late)
         for m in range(CB - 1):

@@ -70,13 +70,16 @@ def tile_transformerencoder_b_kernel(
         for b in range(CB):
             nc.sync.dma_start(table[b][:], in_blocks(emb)[:, b, :])
             load_pos(b, cols(0))
-        load_vector("ln_w", ln_w.rearrange("(p b) o -> p (b o)", b=CB))
-        load_vector("ln_b", ln_b.rearrange("(p b) o -> p (b o)", b=CB))
+            if b == 0:
+                load_vector("ln_w", ln_w.rearrange("(p b) o -> p (b o)", b=CB))
+                load_vector("ln_b", ln_b.rearrange("(p b) o -> p (b o)", b=CB))
         load_weights("q", in_blocks(wq))
-        load_weights("k", in_blocks(wk))
+        load_pos(0, cols(1))
+        load_pos(1, cols(1))
         load_vector("bq", bq.rearrange("(t p) o -> p (t o)", t=H))
-        for b in range(CB):
-            load_pos(b, cols(1))
+        load_weights("k", in_blocks(wk))
+        load_pos(2, cols(1))
+        load_pos(3, cols(1))
         load_weights("v", in_blocks(wv))
         nc.sync.dma_start(bv_row[:], bv.rearrange("c o -> (c o)").partition_broadcast(P))
         load_weights("o", wo.rearrange("(t p) m -> p t m", t=H))
@@ -97,37 +100,45 @@ def tile_transformerencoder_b_kernel(
         x0 = held.tile([P, CB, N], F32, name="x0")
         h = [held.tile([P, N], BF16, name=f"h{b}") for b in range(CB)]
 
-        def mean_over_channels(ps, parts, b, direct, total):
-            if b < direct:
-                nc.tensor.matmul(ps[:], mean_w[:], parts[b], start=(b == 0), stop=(b == CB - 1))
-                return
-            if b > direct:
-                nc.vector.tensor_tensor(
-                    total[:], parts[direct] if b == direct + 1 else total[:], parts[b], ALU.add
-                )
-            if b == CB - 1:
-                nc.tensor.matmul(ps[:], mean_w[:], total[:], start=(direct == 0), stop=True)
-
-        def look_up_and_sum(piece, direct, pool, tag):
+        def look_up_and_sum(piece, pool, tag):
             width = piece.stop - piece.start
             mu_ps = pool.tile([P, width], F32, name="mu_ps", tag=tag)
             m2_ps = pool.tile([P, width], F32, name="m2_ps", tag=tag)
-            sum_x = work.tile([P, width], F32, name="sum_x") if direct < CB else None
-            sum_sq = work.tile([P, width], F32, name="sum_sq") if direct < CB else None
             words = offsets[:, piece.start // 16 : piece.stop // 16]
-            sqs = []
             for b in range(CB):
                 nc.vector.tensor_tensor(
                     x0[:, b, piece], table[b][:].indirect(words), pos_sb[b][:, piece], ALU.add
                 )
                 sq = squares.tile([P, width], F32, name="sq")
                 nc.scalar.activation(sq[:], x0[:, b, piece], ACT.Square)
-                sqs.append(sq[:])
-                mean_over_channels(mu_ps, [x0[:, c, piece] for c in range(CB)], b, direct, sum_x)
-                mean_over_channels(m2_ps, sqs, b, direct, sum_sq)
+                for ps, part in ((mu_ps, x0[:, b, piece]), (m2_ps, sq[:])):
+                    nc.tensor.matmul(ps[:], mean_w[:], part, start=(b == 0), stop=(b == CB - 1))
             return mu_ps, m2_ps
 
-        def normalise(piece, mu_ps, m2_ps):
+        def look_up_and_add(piece, pool, tag):
+            width = piece.stop - piece.start
+            mu_ps = pool.tile([P, width], F32, name="mu_ps", tag=tag)
+            m2_ps = pool.tile([P, width], F32, name="m2_ps", tag=tag)
+            words = offsets[:, piece.start // 16 : piece.stop // 16]
+            sq = squares.tile([P, CB, width], F32, name="sq4", bufs=2)
+            for b in range(CB):
+                nc.vector.tensor_tensor(
+                    x0[:, b, piece], table[b][:].indirect(words), pos_sb[b][:, piece], ALU.add
+                )
+                if b % 2 == 1:
+                    nc.scalar.activation(sq[:, b - 1 : b + 1, :], x0[:, b - 1 : b + 1, piece], ACT.Square)
+            for ps, lower, upper, name in (
+                (mu_ps, x0[:, 0:2, piece], x0[:, 2:4, piece], "sum_x"),
+                (m2_ps, sq[:, 0:2, :], sq[:, 2:4, :], "sum_sq"),
+            ):
+                pair = work.tile([P, 2, width], F32, name=name + "2")
+                nc.vector.tensor_tensor(pair[:], lower, upper, ALU.add)
+                total = work.tile([P, width], F32, name=name)
+                nc.vector.tensor_tensor(total[:], pair[:, 0, :], pair[:, 1, :], ALU.add)
+                nc.tensor.matmul(ps[:], mean_w[:], total[:])
+            return mu_ps, m2_ps
+
+        def normalise(piece, mu_ps, m2_ps, n):
             width = piece.stop - piece.start
             mu_sq = work.tile([P, width], F32, name="mu_sq")
             nc.scalar.activation(mu_sq[:], mu_ps[:], ACT.Square)
@@ -136,14 +147,26 @@ def tile_transformerencoder_b_kernel(
             rstd = work.tile([P, width], F32, name="rstd")
             nc.scalar.activation(rstd[:], var[:], ACT.Abs_reciprocal_sqrt, bias=eps[:])
             xc = work.tile([P, CB, width], F32, name="xc", bufs=2)
+            step = CB if n > 1 else 1
+            for b in range(0, CB, step):
+                nc.vector.tensor_tensor(
+                    xc[:, b : b + step, :],
+                    x0[:, b : b + step, piece],
+                    mu_ps[:].unsqueeze(1).to_broadcast([P, step, width]),
+                    ALU.subtract,
+                )
             for b in range(CB):
-                nc.vector.tensor_tensor(xc[:, b, :], x0[:, b, piece], mu_ps[:], ALU.subtract)
-            for b in range(CB):
-                xn = work.tile([P, width], F32, name="xn")
-                nc.vector.tensor_tensor(xn[:], xc[:, b, :], rstd[:], ALU.mult)
+                if b % n == 0:
+                    xn = work.tile([P, n, width], F32, name=f"xn{n}")
+                    nc.vector.tensor_tensor(
+                        xn[:],
+                        xc[:, b : b + n, :],
+                        rstd[:].unsqueeze(1).to_broadcast([P, n, width]),
+                        ALU.mult,
+                    )
                 nc.scalar.activation(
                     h[b][:, piece],
-                    xn[:],
+                    xn[:, b % n, :],
                     ACT.Identity,
                     bias=per_channel["ln_b"][:, b : b + 1],
                     scale=per_channel["ln_w"][:, b : b + 1],
@@ -152,10 +175,10 @@ def tile_transformerencoder_b_kernel(
         for b in range(CB):
             nc.scalar.mul(table[b][:, 0:S_SCALAR], table[b][:, 0:S_SCALAR], math.sqrt(C))
             nc.vector.tensor_scalar_mul(table[b][:, S_SCALAR:S], table[b][:, S_SCALAR:S], math.sqrt(C))
-        normalise(PIECES[0], *look_up_and_sum(PIECES[0], CB, ctx, "ctx"))
-        normalise(PIECES[1], *look_up_and_sum(PIECES[1], CB, banks, "bank"))
+        normalise(PIECES[0], *look_up_and_sum(PIECES[0], ctx, "ctx"), n=1)
+        normalise(PIECES[1], *look_up_and_sum(PIECES[1], banks, "bank"), n=2)
         for piece in PIECES[2:]:
-            normalise(piece, *look_up_and_sum(piece, 0, ctx, "ctx"))
+            normalise(piece, *look_up_and_add(piece, ctx, "ctx"), n=2)
 
         q = held.tile([P, H, N], BF16, name="q")
         k = held.tile([P, H, N], BF16, name="k")

import math

import concourse.mybir as mybir
from concourse.masks import make_identity

F32 = mybir.dt.float32
BF16 = mybir.dt.bfloat16
U16 = mybir.dt.uint16
ALU = mybir.AluOpType
ACT = mybir.ActivationFunctionType

P = 128
C, S, N, H, DH = 512, 2048, 1024, 4, 128
EPS = 1e-5
CB = C // P
HALF = 512
NH = N // HALF
WIDTH = HALF // 2
PIECES = [slice(j, j + WIDTH) for j in range(0, N, WIDTH)]
HEAD_PAIRS = ((0, 1), (2, 3))
TB = N // P
QB = HALF // P
PAIR = 2
KEYS_A_STEP = TB // QB
S_SCALAR = 640
FLOPS = 2 * (4 * C * C * N + 2 * H * N * N * DH)


def tile_transformerencoder_b_kernel(
    tc, emb, pos, ln_w, ln_b, wq, bq, wk, wv, bv, wo, bo, offs, out
):
    nc = tc.nc
    with (
        tc.tile_pool(name="lists", bufs=1) as lists,
        tc.tile_pool(name="held", bufs=1) as held,
        tc.tile_pool(name="work", bufs=3) as work,
        tc.tile_pool(name="squares", bufs=CB) as squares,
        tc.tile_pool(name="stores", bufs=CB + 1) as stores,
        tc.tile_pool(name="probs", bufs=2) as probs,
        tc.psum_pool(name="banks", bufs=5) as banks,
        tc.psum_pool(name="ctx", bufs=2) as ctx,
        tc.psum_pool(name="flip", bufs=1) as flip,
    ):
        def cols(s):
            return slice(s * HALF, (s + 1) * HALF)

        offsets = lists.tile([P, N // 16], U16, name="offsets")
        nc.sync.dma_start(offsets[:], offs)

        table = [held.tile([P, S], F32, name=f"table{b}") for b in range(CB)]
        pos_sb = [held.tile([P, N], F32, name=f"pos{b}") for b in range(CB)]
        weights = {name: held.tile([P, CB, C], BF16, name=f"w{name}") for name in "qkvo"}
        bv_row = held.tile([P, C], F32, name="bv_row")

        def in_blocks(x):
            return x.rearrange("(p b) n -> p b n", b=CB)

        def load_pos(b, piece):
            nc.sync.dma_start(pos_sb[b][:, piece], in_blocks(pos)[:, b, piece])

        def load_weights(name, w):
            nc.sync.dma_start(weights[name][:], w)

        def load_vector(name, columns):
            per_channel[name] = held.tile([P, CB], F32, name=name)
            with nc.allow_non_contiguous_dma(reason="512 floats, four to a partition"):
                nc.sync.dma_start(per_channel[name][:], columns)

        per_channel = {}
        for b in range(CB):
            nc.sync.dma_start(table[b][:], in_blocks(emb)[:, b, :])
            load_pos(b, cols(0))
            if b == 0:
                load_vector("ln_w", ln_w.rearrange("(p b) o -> p (b o)", b=CB))
                load_vector("ln_b", ln_b.rearrange("(p b) o -> p (b o)", b=CB))
        load_weights("q", in_blocks(wq))
        load_pos(0, cols(1))
        load_pos(1, cols(1))
        load_vector("bq", bq.rearrange("(t p) o -> p (t o)", t=H))
        load_weights("k", in_blocks(wk))
        load_pos(2, cols(1))
        load_pos(3, cols(1))
        load_weights("v", in_blocks(wv))
        nc.sync.dma_start(bv_row[:], bv.rearrange("c o -> (c o)").partition_broadcast(P))
        load_weights("o", wo.rearrange("(t p) m -> p t m", t=H))
        load_vector("bo", bo.rearrange("(p b) o -> p (b o)", b=CB))

        mean_w = held.tile([P, P], F32, name="mean_w")
        nc.vector.memset(mean_w[:], 1.0 / C)
        eps = held.tile([P, 1], F32, name="eps")
        nc.vector.memset(eps[:], EPS)
        first = held.tile([P, 1], F32, name="first")
        nc.scalar.activation(first[:], eps[:], ACT.Abs_reciprocal_sqrt)
        ident = held.tile([P, P], BF16, name="ident")
        make_identity(nc, ident[:])
        v_aug = [held.tile([P, H, DH + 1], BF16, name=f"v_aug{i}") for i in range(TB)]
        for i in range(TB):
            nc.gpsimd.memset(v_aug[i][:], 1.0)

        x0 = held.tile([P, CB, N], F32, name="x0")
        h = [held.tile([P, N], BF16, name=f"h{b}") for b in range(CB)]

        def look_up_and_sum(piece, pool, tag):
            width = piece.stop - piece.start
            mu_ps = pool.tile([P, width], F32, name="mu_ps", tag=tag)
            m2_ps = pool.tile([P, width], F32, name="m2_ps", tag=tag)
            words = offsets[:, piece.start // 16 : piece.stop // 16]
            for b in range(CB):
                nc.vector.tensor_tensor(
                    x0[:, b, piece], table[b][:].indirect(words), pos_sb[b][:, piece], ALU.add
                )
                sq = squares.tile([P, width], F32, name="sq")
                nc.scalar.activation(sq[:], x0[:, b, piece], ACT.Square)
                for ps, part in ((mu_ps, x0[:, b, piece]), (m2_ps, sq[:])):
                    nc.tensor.matmul(ps[:], mean_w[:], part, start=(b == 0), stop=(b == CB - 1))
            return mu_ps, m2_ps

        def look_up_and_add(piece, pool, tag):
            width = piece.stop - piece.start
            mu_ps = pool.tile([P, width], F32, name="mu_ps", tag=tag)
            m2_ps = pool.tile([P, width], F32, name="m2_ps", tag=tag)
            words = offsets[:, piece.start // 16 : piece.stop // 16]
            sq = squares.tile([P, CB, width], F32, name="sq4", bufs=2)
            for b in range(CB):
                nc.vector.tensor_tensor(
                    x0[:, b, piece], table[b][:].indirect(words), pos_sb[b][:, piece], ALU.add
                )
                if b % 2 == 1:
                    nc.scalar.activation(sq[:, b - 1 : b + 1, :], x0[:, b - 1 : b + 1, piece], ACT.Square)
            for ps, lower, upper, name in (
                (mu_ps, x0[:, 0:2, piece], x0[:, 2:4, piece], "sum_x"),
                (m2_ps, sq[:, 0:2, :], sq[:, 2:4, :], "sum_sq"),
            ):
                pair = work.tile([P, 2, width], F32, name=name + "2")
                nc.vector.tensor_tensor(pair[:], lower, upper, ALU.add)
                total = work.tile([P, width], F32, name=name)
                nc.vector.tensor_tensor(total[:], pair[:, 0, :], pair[:, 1, :], ALU.add)
                nc.tensor.matmul(ps[:], mean_w[:], total[:])
            return mu_ps, m2_ps

        def normalise(piece, mu_ps, m2_ps, n):
            width = piece.stop - piece.start
            mu_sq = work.tile([P, width], F32, name="mu_sq")
            nc.scalar.activation(mu_sq[:], mu_ps[:], ACT.Square)
            var = work.tile([P, width], F32, name="var")
            nc.vector.tensor_tensor(var[:], m2_ps[:], mu_sq[:], ALU.subtract)
            rstd = work.tile([P, width], F32, name="rstd")
            nc.scalar.activation(rstd[:], var[:], ACT.Abs_reciprocal_sqrt, bias=eps[:])
            xc = work.tile([P, CB, width], F32, name="xc", bufs=2)
            step = CB if n > 1 else 1
            for b in range(0, CB, step):
                nc.vector.tensor_tensor(
                    xc[:, b : b + step, :],
                    x0[:, b : b + step, piece],
                    mu_ps[:].unsqueeze(1).to_broadcast([P, step, width]),
                    ALU.subtract,
                )
            for b in range(CB):
                if b % n == 0:
                    xn = work.tile([P, n, width], F32, name=f"xn{n}")
                    nc.vector.tensor_tensor(
                        xn[:],
                        xc[:, b : b + n, :],
                        rstd[:].unsqueeze(1).to_broadcast([P, n, width]),
                        ALU.mult,
                    )
                nc.scalar.activation(
                    h[b][:, piece],
                    xn[:, b % n, :],
                    ACT.Identity,
                    bias=per_channel["ln_b"][:, b : b + 1],
                    scale=per_channel["ln_w"][:, b : b + 1],
                )

        for b in range(CB):
            nc.scalar.mul(table[b][:, 0:S_SCALAR], table[b][:, 0:S_SCALAR], math.sqrt(C))
            nc.vector.tensor_scalar_mul(table[b][:, S_SCALAR:S], table[b][:, S_SCALAR:S], math.sqrt(C))
        normalise(PIECES[0], *look_up_and_sum(PIECES[0], ctx, "ctx"), n=1)
        normalise(PIECES[1], *look_up_and_sum(PIECES[1], banks, "bank"), n=2)
        for piece in PIECES[2:]:
            normalise(piece, *look_up_and_add(piece, ctx, "ctx"), n=2)

        q = held.tile([P, H, N], BF16, name="q")
        k = held.tile([P, H, N], BF16, name="k")
        o = [held.tile([P, N], BF16, name=f"o{t}") for t in range(H)]

        def project(w, heads, piece):
            ps = banks.tile([P, len(heads), piece.stop - piece.start], F32, name="proj_ps", tag="bank")
            for n, t in enumerate(heads):
                for b in range(CB):
                    nc.tensor.matmul(
                        ps[:, n, :],
                        w[:, b, t * DH : (t + 1) * DH],
                        h[b][:, piece],
                        start=(b == 0),
                        stop=(b == CB - 1),
                    )
            return ps

        def project_k(heads, piece):
            ps = project(weights["k"], heads, piece)
            out_k = k[:, heads[0] : heads[-1] + 1, piece]
            if piece.stop < N:
                nc.scalar.copy(out_k, ps[:])
            else:
                nc.vector.tensor_copy(out_k, ps[:])

        def project_q(heads, piece):
            ps = project(weights["q"], heads, piece)
            for n, t in enumerate(heads):
                bias = per_channel["bq"][:, t : t + 1]
                if piece.stop < N:
                    nc.scalar.activation(q[:, t, piece], ps[:, n, :], ACT.Identity, bias=bias)
                else:
                    nc.vector.tensor_scalar_add(q[:, t, piece], ps[:, n, :], bias)

        def project_v(i):
            ps = banks.tile([P, C], F32, name="v_ps", tag="bank")
            for b in range(CB):
                nc.tensor.matmul(
                    ps[:],
                    h[b][:, i * P : (i + 1) * P],
                    weights["v"][:, b, :],
                    start=(b == 0),
                    stop=(b == CB - 1),
                )
            nc.vector.tensor_tensor(
                v_aug[i][:, :, 0:DH],
                ps[:].rearrange("p (t d) -> p t d", t=H),
                bv_row[:].rearrange("p (t d) -> p t d", t=H),
                ALU.add,
            )

        def exp_scores(t, s, i, e):
            ps = banks.tile([P, HALF], F32, name="sc_ps", tag="bank")
            nc.tensor.matmul(
                ps[:], k[:, t, i * P : (i + 1) * P], q[:, t, cols(s)], start=True, stop=True
            )
            nc.scalar.activation(e[:, i, :], ps[:], ACT.Exp, scale=1.0 / math.sqrt(DH))

        def attend(ps, t, j, e):
            for i in range(TB):
                nc.tensor.matmul(
                    ps[:, j % PAIR, :],
                    e[:, i, j * P : (j + 1) * P],
                    v_aug[i][:, t, :],
                    start=(i == 0),
                    stop=(i == TB - 1),
                )

        def divide(ps):
            rsum = work.tile([P, PAIR, 1], F32, name="rsum")
            nc.vector.reciprocal(rsum[:], ps[:, :, DH : DH + 1])
            o_tok = work.tile([P, PAIR, DH], BF16, name="o_tok")
            nc.vector.tensor_tensor(
                o_tok[:], ps[:, :, 0:DH], rsum[:].to_broadcast([P, PAIR, DH]), ALU.mult
            )
            return o_tok

        def flip_back(o_tok, t, s, first, flip_ps):
            for n in range(PAIR):
                j = first + n
                nc.tensor.transpose(flip_ps[:, j * P : (j + 1) * P], o_tok[:, n, :], ident[:])
            if first + PAIR == QB:
                nc.vector.tensor_copy(o[t][:, cols(s)], flip_ps[:])

        def project_out(m, tokens):
            width = tokens.stop - tokens.start
            ps = banks.tile([P, width], F32, name="y_ps", tag="bank")
            for t in range(H):
                nc.tensor.matmul(
                    ps[:],
                    weights["o"][:, t, m::CB],
                    o[t][:, tokens],
                    start=(t == 0),
                    stop=(t == H - 1),
                )
            y = stores.tile([P, width], F32, name="y")
            nc.vector.scalar_tensor_tensor(
                y[:], ps[:], per_channel["bo"][:, m : m + 1], x0[:, m, tokens], ALU.add, ALU.add
            )
            nc.sync.dma_start(in_blocks(out)[:, m, tokens], y[:])

        groups = [(t, s) for s in range(NH) for t in range(H)]
        last = len(groups) - 1

        def between_rounds(g):
            if g in (0, 2):
                project_q(HEAD_PAIRS[g // 2], PIECES[3])
            if g >= H:
                project_out(g - H, cols(0))

        for piece in PIECES[:2]:
            for heads in HEAD_PAIRS:
                project_q(heads, piece)
                project_k(heads, piece)
            for i in range(piece.start // P, piece.stop // P):
                project_v(i)
        for heads in HEAD_PAIRS:
            project_k(heads, PIECES[2])
        for heads in HEAD_PAIRS:
            project_q(heads, PIECES[2])
        e_next = probs.tile([P, TB, HALF], BF16, name="e")
        for i in range(TB):
            exp_scores(0, 0, i, e_next)
            if i < 2:
                project_v(QB + i)
            elif i < 4:
                project_k(HEAD_PAIRS[i - 2], PIECES[3])
            elif i < 6:
                project_v(QB + i - 2)

        late = None
        for g, (t, s) in enumerate(groups):
            e_now = e_next
            if g < last:
                t_next, s_next = groups[g + 1]
                e_next = probs.tile([P, TB, HALF], BF16, name="e")
            for j in range(QB):
                if g < last:
                    for i in range(KEYS_A_STEP * j, KEYS_A_STEP * (j + 1)):
                        exp_scores(t_next, s_next, i, e_next)
                if j % PAIR == 0:
                    ps = ctx.tile([P, PAIR, DH + 1], F32, name="ctx_ps", tag="ctx")
                attend(ps, t, j, e_now)
                if j % PAIR == PAIR - 1:
                    if late is not None:
                        flip_back(*late)
                    if j == PAIR - 1:
                        flip_ps = flip.tile([P, HALF], BF16, name="flip_ps", tag="flip")
                    late = (divide(ps), t, s, j + 1 - PAIR, flip_ps)
            between_rounds(g)
        flip_back(*late)
        for m in range(CB - 1):
            project_out(m, cols(1))
        project_out(CB - 1, slice(HALF, HALF + HALF // 2))
        project_out(CB - 1, slice(HALF + HALF // 2, N))
